import numpy as np
import ml_dtypes


def mxq(x, axis, fmt="e4m3"):
    dtype, down = {"e4m3": (ml_dtypes.float8_e4m3fn, 7), "e5m2": (ml_dtypes.float8_e5m2, 14)}[fmt]
    v = np.moveaxis(np.asarray(x, np.float32).astype(ml_dtypes.bfloat16).astype(np.float64), axis, -1)
    blocks = v.reshape(v.shape[:-1] + (-1, 32))
    amax = np.abs(blocks).max(-1, keepdims=True)
    byte = np.maximum(np.where(amax > 0, np.frexp(amax)[1] - 1 + 127, 0) - down, 1)
    scale = np.exp2(byte - 127.0)
    codes = (blocks / scale).astype(np.float32).astype(dtype).astype(np.float64)
    return np.moveaxis((codes * scale).reshape(v.shape), -1, axis)


WIDE = False


def mx_kscale(k):
    if not WIDE:
        return np.ones(k)
    levels = np.array([10, -10, 5, -5, 0])
    a = np.random.permutation(np.resize(levels, k // 512 * 4)).reshape(k // 512, 4)
    idx = np.arange(k)
    return np.exp2(a[idx // 512, idx % 128 // 32])


BF16 = ml_dtypes.bfloat16


def bf(x):
    return np.asarray(x, np.float32).astype(BF16)


def f64(x):
    return np.asarray(x).astype(np.float64)


M, K, N = 1536, 1536, 1536


def setup_inputs():
    s = mx_kscale(K)
    return {"A": bf(np.random.standard_normal((M, K)) * s),
            "B": bf(np.random.standard_normal((K, N)) * 2.0 / np.sqrt(K) / s[:, None])}


def reference(A, B):
    C = mxq(np.tril(f64(A)), 1, "e4m3") @ mxq(np.tril(f64(B)), 0, "e4m3")
    return np.tril(C)

@@ -1,0 +1,161 @@
+from contextlib import ExitStack
+
+import concourse.mybir as mybir
+from concourse.masks import make_identity
+
+BF16 = mybir.dt.bfloat16
+F32 = mybir.dt.float32
+I32 = mybir.dt.int32
+U32 = mybir.dt.uint32
+U8 = mybir.dt.uint8
+FP8X4 = mybir.dt.float8_e4m3fn_x4
+ALU = mybir.AluOpType
+
+SIZE = 1536
+P = 128
+K_PASS = 512
+HALF = 256
+ROW_BLOCKS = SIZE // P
+PASSES = SIZE // K_PASS
+BLOCKS_PER_PASS = K_PASS // P
+
+FLOPS = 2 * (SIZE * (SIZE + 1) * (SIZE + 2) // 6)
+BYTES = 2 * (SIZE * (SIZE + 1) // 2) * 2 + SIZE * SIZE * 4
+
+
+def tile_modelnew_kernel(tc, A, B, out):
+    nc = tc.nc
+    with ExitStack() as ctx:
+        const = ctx.enter_context(tc.tile_pool(name="const", bufs=1))
+        keep = ctx.enter_context(tc.tile_pool(name="keep", bufs=1))
+        stage = ctx.enter_context(tc.tile_pool(name="stage", bufs=3))
+        psum_t = ctx.enter_context(tc.psum_pool(name="psum_t", bufs=3))
+        psum_o = ctx.enter_context(tc.psum_pool(name="psum_o", bufs=5))
+
+        raw_a = []
+        for mi in range(ROW_BLOCKS):
+            width = K_PASS * (mi // BLOCKS_PER_PASS + 1)
+            raw_a.append(keep.tile([P, width], BF16, name="raw_a%d" % mi, align_bytes=64))
+        raw_b = []
+        codes_b = []
+        scales_b = []
+        for c in range(PASSES):
+            width = K_PASS * (c + 1)
+            raw_b.append(keep.tile([P, 4, width], BF16, name="raw_b%d" % c, align_bytes=64))
+            codes_b.append(keep.tile([P, width], U32, name="codes_b%d" % c, align_bytes=64))
+            scales_b.append(keep.tile([P, width], U8, name="scales_b%d" % c, align_bytes=64))
+        units = [(mi, c) for mi in range(ROW_BLOCKS) for c in range(mi // BLOCKS_PER_PASS + 1)]
+        unit_of = dict((u, i) for i, u in enumerate(units))
+        codes_a = keep.tile([P, len(units), P], U32, name="codes_a", align_bytes=64)
+        scales_a = keep.tile([P, len(units), P], U8, name="scales_a", align_bytes=64)
+        out_sb = [keep.tile([P, SIZE], F32, name="out_sb%d" % mi) for mi in range(ROW_BLOCKS)]
+
+        for g in range(PASSES):
+            width = K_PASS * (g + 1)
+            for u in range(2):
+                cols = width - HALF * (1 - u)
+                rows = B[K_PASS * g + HALF * u : K_PASS * g + HALF * (u + 1), 0:cols]
+                nc.sync.dma_start(
+                    out=raw_b[g][:, 2 * u : 2 * u + 2, 0:cols],
+                    in_=rows.rearrange("(q e) w -> q e w", e=2),
+                )
+            for r in range(BLOCKS_PER_PASS):
+                mi = BLOCKS_PER_PASS * g + r
+                cols = P * (mi + 1)
+                nc.sync.dma_start(out=raw_a[mi][:, 0:cols], in_=A[P * mi : P * (mi + 1), 0:cols])
+
+        ident = const.tile([P, P], F32, name="ident")
+        make_identity(nc, ident[:])
+        mask_a_f = const.tile([P, P // 2], F32, name="mask_a_f")
+        mask_b_f = const.tile([P, 2, P], F32, name="mask_b_f")
+        nc.gpsimd.memset(mask_a_f[:], -1.0)
+        nc.gpsimd.memset(mask_b_f[:], -1.0)
+        for base, fill in ((-1, 65535.0), (0, 0.0)):
+            nc.gpsimd.affine_select(
+                out=mask_a_f[:], in_=mask_a_f[:], compare_op=ALU.is_ge, fill=fill,
+                base=base, pattern=[[-2, P // 2]], channel_multiplier=1,
+            )
+            nc.gpsimd.affine_select(
+                out=mask_b_f[:], in_=mask_b_f[:], compare_op=ALU.is_ge, fill=fill,
+                base=base, pattern=[[1, 2], [-2, P]], channel_multiplier=2,
+            )
+        mask_a = const.tile([P, P // 2], I32, name="mask_a")
+        mask_b = const.tile([P, 2, P], I32, name="mask_b")
+        nc.vector.tensor_copy(out=mask_a[:], in_=mask_a_f[:])
+        nc.vector.tensor_copy(out=mask_b[:], in_=mask_b_f[:])
+
+        for g in range(PASSES):
+            width = K_PASS * (g + 1)
+            nc.vector.memset(raw_b[g][:].bitcast(I32)[:, 0:2, (width - HALF) // 2 :], 0)
+            for r in range(BLOCKS_PER_PASS - 1):
+                mi = BLOCKS_PER_PASS * g + r
+                nc.vector.memset(raw_a[mi][:].bitcast(I32)[:, P * (mi + 1) // 2 :], 0)
+
+        for g in range(PASSES):
+            width = K_PASS * (g + 1)
+            b_words = raw_b[g][:].bitcast(I32)
+            for u in range(2):
+                lo = (K_PASS * g + HALF * u) // 2
+                diag = b_words[:, 2 * u : 2 * u + 2, lo : lo + P]
+                nc.vector.tensor_tensor(out=diag, in0=diag, in1=mask_b[:], op=ALU.bitwise_and)
+            for j in range(g + 1):
+                cols = slice(K_PASS * j, K_PASS * (j + 1))
+                grouped_b = stage.tile([P, 4 * K_PASS], BF16, name="grouped_b", align_bytes=64)
+                nc.vector.tensor_copy(
+                    out=grouped_b[:].rearrange("p (c i t) -> p c t i", i=4, t=4),
+                    in_=raw_b[g][:, :, cols].rearrange("p t (c i) -> p c t i", i=4),
+                )
+                nc.vector.quantize_mx(
+                    out=codes_b[g][:, cols].bitcast(FP8X4),
+                    scales=scales_b[g][:, cols],
+                    in_=grouped_b[:],
+                )
+            group_units = [u for u in units if u[0] // BLOCKS_PER_PASS == g]
+            for r in range(BLOCKS_PER_PASS):
+                mi = BLOCKS_PER_PASS * g + r
+                diag = raw_a[mi][:].bitcast(I32)[:, P * mi // 2 : P * (mi + 1) // 2]
+                nc.vector.tensor_tensor(out=diag, in0=diag, in1=mask_a[:], op=ALU.bitwise_and)
+            for first in range(0, len(group_units), 2):
+                pair = group_units[first : first + 2]
+                xt = psum_t.tile([P, 2, 2, P], F32, name="xt")
+                for a, (mi, c) in enumerate(pair):
+                    a_words = raw_a[mi][:].bitcast(F32)
+                    for u in range(2):
+                        lo = (K_PASS * c + HALF * u) // 2
+                        nc.tensor.transpose(xt[:, a, u, :], a_words[:, lo : lo + P], ident[:])
+                grouped_a = stage.tile([P, 2 * K_PASS], BF16, name="grouped_a", align_bytes=64)
+                nc.scalar.copy(
+                    out=grouped_a[:].bitcast(F32).rearrange("p (a m u) -> p a m u", a=2, u=2),
+                    in_=xt[:].rearrange("p a u m -> p a m u"),
+                )
+                i0 = unit_of[pair[0]]
+                nc.vector.quantize_mx(
+                    out=codes_a[:, i0 : i0 + 2, :].rearrange("p a m -> p (a m)").bitcast(FP8X4),
+                    scales=scales_a[:, i0 : i0 + 2, :].rearrange("p a m -> p (a m)"),
+                    in_=grouped_a[:],
+                )
+            for r in range(BLOCKS_PER_PASS):
+                mi = BLOCKS_PER_PASS * g + r
+                kept = P * (mi + 1)
+                if kept < SIZE:
+                    nc.vector.memset(out_sb[mi][:, kept:], 0.0)
+                for n in range(g + 1):
+                    need = min(K_PASS, kept - K_PASS * n)
+                    wide = need if need in (128, 256, 512) else K_PASS
+                    acc = psum_o.tile([P, K_PASS], F32, name="acc")
+                    for c in range(n, g + 1):
+                        i = unit_of[(mi, c)]
+                        cols = slice(K_PASS * n, K_PASS * n + wide)
+                        nc.tensor.matmul_mx(
+                            out=acc[:, 0:wide],
+                            lhsT=codes_a[:, i, :].bitcast(FP8X4),
+                            lhsT_scale=scales_a[:, i, :],
+                            rhs=codes_b[c][:, cols].bitcast(FP8X4),
+                            rhs_scale=scales_b[c][:, cols],
+                            start=(c == n),
+                            stop=(c == g),
+                        )
+                    nc.scalar.copy(
+                        out=out_sb[mi][:, K_PASS * n : K_PASS * n + need], in_=acc[:, 0:need]
+                    )
+                nc.sync.dma_start(out=out[P * mi : P * (mi + 1), :], in_=out_sb[mi][:])

@@ -28,9 +28,10 @@ def tile_modelnew_kernel(tc, A, B, out):
     with ExitStack() as ctx:
         const = ctx.enter_context(tc.tile_pool(name="const", bufs=1))
         keep = ctx.enter_context(tc.tile_pool(name="keep", bufs=1))
-        stage = ctx.enter_context(tc.tile_pool(name="stage", bufs=3))
-        psum_t = ctx.enter_context(tc.psum_pool(name="psum_t", bufs=3))
-        psum_o = ctx.enter_context(tc.psum_pool(name="psum_o", bufs=5))
+        stage_b = ctx.enter_context(tc.tile_pool(name="stage_b", bufs=3))
+        stage_a = ctx.enter_context(tc.tile_pool(name="stage_a", bufs=6))
+        psum = ctx.enter_context(tc.psum_pool(name="psum", bufs=8))
+        ctx.enter_context(tc.manual_schedule())
 
         raw_a = []
         for mi in range(ROW_BLOCKS):
@@ -45,12 +46,23 @@ def tile_modelnew_kernel(tc, A, B, out):
             codes_b.append(keep.tile([P, width], U32, name="codes_b%d" % c, align_bytes=64))
             scales_b.append(keep.tile([P, width], U8, name="scales_b%d" % c, align_bytes=64))
         units = [(mi, c) for mi in range(ROW_BLOCKS) for c in range(mi // BLOCKS_PER_PASS + 1)]
-        unit_of = dict((u, i) for i, u in enumerate(units))
+        unit_of = dict((unit, i) for i, unit in enumerate(units))
         codes_a = keep.tile([P, len(units), P], U32, name="codes_a", align_bytes=64)
         scales_a = keep.tile([P, len(units), P], U8, name="scales_a", align_bytes=64)
-        out_sb = [keep.tile([P, SIZE], F32, name="out_sb%d" % mi) for mi in range(ROW_BLOCKS)]
+        out_sb = [keep.tile([P, SIZE], F32, name="out_sb%d" % mi) for mi in range(8)]
+        out_sb.extend(out_sb[0:4])
+        ident = const.tile([P, P], F32, name="ident")
+        zero_src = const.tile([P, 8], F32, name="zero_src")
+        mask_a_f = const.tile([P, P // 2], F32, name="mask_a_f")
+        mask_b_f = const.tile([P, 2, P], F32, name="mask_b_f")
+        mask_a = const.tile([P, P // 2], I32, name="mask_a")
+        mask_b = const.tile([P, 2, P], I32, name="mask_b")
+        grouped_b = {}
+        grouped_a = {}
+        banks_t = {}
+        banks_o = {}
 
-        for g in range(PASSES):
+        def load_b(g):
             width = K_PASS * (g + 1)
             for u in range(2):
                 cols = width - HALF * (1 - u)
@@ -59,103 +71,221 @@ def tile_modelnew_kernel(tc, A, B, out):
                     out=raw_b[g][:, 2 * u : 2 * u + 2, 0:cols],
                     in_=rows.rearrange("(q e) w -> q e w", e=2),
                 )
-            for r in range(BLOCKS_PER_PASS):
-                mi = BLOCKS_PER_PASS * g + r
-                cols = P * (mi + 1)
-                nc.sync.dma_start(out=raw_a[mi][:, 0:cols], in_=A[P * mi : P * (mi + 1), 0:cols])
 
-        ident = const.tile([P, P], F32, name="ident")
-        make_identity(nc, ident[:])
-        mask_a_f = const.tile([P, P // 2], F32, name="mask_a_f")
-        mask_b_f = const.tile([P, 2, P], F32, name="mask_b_f")
-        nc.gpsimd.memset(mask_a_f[:], -1.0)
-        nc.gpsimd.memset(mask_b_f[:], -1.0)
-        for base, fill in ((-1, 65535.0), (0, 0.0)):
-            nc.gpsimd.affine_select(
-                out=mask_a_f[:], in_=mask_a_f[:], compare_op=ALU.is_ge, fill=fill,
-                base=base, pattern=[[-2, P // 2]], channel_multiplier=1,
-            )
-            nc.gpsimd.affine_select(
-                out=mask_b_f[:], in_=mask_b_f[:], compare_op=ALU.is_ge, fill=fill,
-                base=base, pattern=[[1, 2], [-2, P]], channel_multiplier=2,
-            )
-        mask_a = const.tile([P, P // 2], I32, name="mask_a")
-        mask_b = const.tile([P, 2, P], I32, name="mask_b")
-        nc.vector.tensor_copy(out=mask_a[:], in_=mask_a_f[:])
-        nc.vector.tensor_copy(out=mask_b[:], in_=mask_b_f[:])
+        def load_a(mi):
+            cols = P * (mi + 1)
+            nc.sync.dma_start(out=raw_a[mi][:, 0:cols], in_=A[P * mi : P * (mi + 1), 0:cols])
 
-        for g in range(PASSES):
+        def zero_b(g):
             width = K_PASS * (g + 1)
             nc.vector.memset(raw_b[g][:].bitcast(I32)[:, 0:2, (width - HALF) // 2 :], 0)
-            for r in range(BLOCKS_PER_PASS - 1):
-                mi = BLOCKS_PER_PASS * g + r
-                nc.vector.memset(raw_a[mi][:].bitcast(I32)[:, P * (mi + 1) // 2 :], 0)
 
-        for g in range(PASSES):
-            width = K_PASS * (g + 1)
-            b_words = raw_b[g][:].bitcast(I32)
-            for u in range(2):
-                lo = (K_PASS * g + HALF * u) // 2
-                diag = b_words[:, 2 * u : 2 * u + 2, lo : lo + P]
-                nc.vector.tensor_tensor(out=diag, in0=diag, in1=mask_b[:], op=ALU.bitwise_and)
-            for j in range(g + 1):
-                cols = slice(K_PASS * j, K_PASS * (j + 1))
-                grouped_b = stage.tile([P, 4 * K_PASS], BF16, name="grouped_b", align_bytes=64)
-                nc.vector.tensor_copy(
-                    out=grouped_b[:].rearrange("p (c i t) -> p c t i", i=4, t=4),
-                    in_=raw_b[g][:, :, cols].rearrange("p t (c i) -> p c t i", i=4),
+        def zero_a(mi):
+            nc.vector.memset(raw_a[mi][:].bitcast(I32)[:, P * (mi + 1) // 2 :], 0)
+
+        def zero_out_scalar(mi):
+            kept = P * (mi + 1)
+            nc.scalar.copy(
+                out=out_sb[mi][:, kept:], in_=zero_src[:, 0:1].to_broadcast([P, SIZE - kept])
+            )
+
+        def zero_out_vector(mi):
+            nc.vector.memset(out_sb[mi][:, P * (mi + 1) :], 0.0)
+
+        def mask_b_half(g, u):
+            lo = (K_PASS * g + HALF * u) // 2
+            diag = raw_b[g][:].bitcast(I32)[:, 2 * u : 2 * u + 2, lo : lo + P]
+            nc.vector.tensor_tensor(out=diag, in0=diag, in1=mask_b[:], op=ALU.bitwise_and)
+
+        def regroup_b(g, j, on_scalar=False):
+            cols = slice(K_PASS * j, K_PASS * (j + 1))
+            grouped = stage_b.tile([P, 4 * K_PASS], BF16, name="grouped_b", align_bytes=64)
+            grouped_b[(g, j)] = grouped
+            dst = grouped[:].rearrange("p (c i t) -> p c t i", i=4, t=4)
+            src = raw_b[g][:, :, cols].rearrange("p t (c i) -> p c t i", i=4)
+            if on_scalar:
+                nc.scalar.copy(out=dst, in_=src)
+            else:
+                nc.vector.tensor_copy(out=dst, in_=src)
+
+        def quant_b(g, j):
+            cols = slice(K_PASS * j, K_PASS * (j + 1))
+            nc.vector.quantize_mx(
+                out=codes_b[g][:, cols].bitcast(FP8X4),
+                scales=scales_b[g][:, cols],
+                in_=grouped_b[(g, j)][:],
+            )
+
+        def mask_a_block(mi):
+            diag = raw_a[mi][:].bitcast(I32)[:, P * mi // 2 : P * (mi + 1) // 2]
+            nc.vector.tensor_tensor(out=diag, in0=diag, in1=mask_a[:], op=ALU.bitwise_and)
+
+        def transpose_pair(pair):
+            xt = psum.tile([P, 2, 2, P], F32, name="xt", tag="bank")
+            banks_t[pair] = xt
+            for a in range(2):
+                mi, c = units[2 * pair + a]
+                a_words = raw_a[mi][:].bitcast(F32)
+                for u in range(2):
+                    lo = (K_PASS * c + HALF * u) // 2
+                    nc.tensor.transpose(xt[:, a, u, :], a_words[:, lo : lo + P], ident[:])
+
+        def copy_pair(pair, on_vector=False):
+            grouped = stage_a.tile([P, 2 * K_PASS], BF16, name="grouped_a", align_bytes=64)
+            grouped_a[pair] = grouped
+            dst = grouped[:].bitcast(F32).rearrange("p (a m u) -> p a m u", a=2, u=2)
+            src = banks_t[pair][:].rearrange("p a u m -> p a m u")
+            if on_vector:
+                nc.vector.tensor_copy(out=dst, in_=src)
+            else:
+                nc.scalar.copy(out=dst, in_=src)
+
+        def quant_pair(pair):
+            i0 = 2 * pair
+            nc.vector.quantize_mx(
+                out=codes_a[:, i0 : i0 + 2, :].rearrange("p a m -> p (a m)").bitcast(FP8X4),
+                scales=scales_a[:, i0 : i0 + 2, :].rearrange("p a m -> p (a m)"),
+                in_=grouped_a[pair][:],
+            )
+
+        def passes(mi, n, first, last):
+            g = mi // BLOCKS_PER_PASS
+            need = min(K_PASS, P * (mi + 1) - K_PASS * n)
+            wide = need if need in (128, 256, 512) else K_PASS
+            if first == n:
+                acc = psum.tile([P, K_PASS], F32, name="acc", tag="bank")
+                banks_o[(mi, n)] = acc
+            acc = banks_o[(mi, n)]
+            cols = slice(K_PASS * n, K_PASS * n + wide)
+            for c in range(first, last + 1):
+                i = unit_of[(mi, c)]
+                nc.tensor.matmul_mx(
+                    out=acc[:, 0:wide],
+                    lhsT=codes_a[:, i, :].bitcast(FP8X4),
+                    lhsT_scale=scales_a[:, i, :],
+                    rhs=codes_b[c][:, cols].bitcast(FP8X4),
+                    rhs_scale=scales_b[c][:, cols],
+                    start=(c == n),
+                    stop=(c == g),
                 )
-                nc.vector.quantize_mx(
-                    out=codes_b[g][:, cols].bitcast(FP8X4),
-                    scales=scales_b[g][:, cols],
-                    in_=grouped_b[:],
+
+        def copy_out(mi, n, on_vector=False):
+            need = min(K_PASS, P * (mi + 1) - K_PASS * n)
+            dst = out_sb[mi][:, K_PASS * n : K_PASS * n + need]
+            if on_vector:
+                nc.vector.tensor_copy(out=dst, in_=banks_o[(mi, n)][:, 0:need])
+            else:
+                nc.scalar.copy(out=dst, in_=banks_o[(mi, n)][:, 0:need])
+
+        def store(mi):
+            nc.sync.dma_start(out=out[P * mi : P * (mi + 1), :], in_=out_sb[mi][:])
+
+        def products(mi):
+            g = mi // BLOCKS_PER_PASS
+            for n in range(g + 1):
+                passes(mi, n, n, g)
+                copy_out(mi, n)
+            store(mi)
+
+        def build_masks():
+            nc.gpsimd.memset(mask_b_f[:], -1.0)
+            for base, fill in ((-1, 65535.0), (0, 0.0)):
+                nc.gpsimd.affine_select(
+                    out=mask_b_f[:], in_=mask_b_f[:], compare_op=ALU.is_ge, fill=fill,
+                    base=base, pattern=[[1, 2], [-2, P]], channel_multiplier=2,
                 )
-            group_units = [u for u in units if u[0] // BLOCKS_PER_PASS == g]
-            for r in range(BLOCKS_PER_PASS):
-                mi = BLOCKS_PER_PASS * g + r
-                diag = raw_a[mi][:].bitcast(I32)[:, P * mi // 2 : P * (mi + 1) // 2]
-                nc.vector.tensor_tensor(out=diag, in0=diag, in1=mask_a[:], op=ALU.bitwise_and)
-            for first in range(0, len(group_units), 2):
-                pair = group_units[first : first + 2]
-                xt = psum_t.tile([P, 2, 2, P], F32, name="xt")
-                for a, (mi, c) in enumerate(pair):
-                    a_words = raw_a[mi][:].bitcast(F32)
-                    for u in range(2):
-                        lo = (K_PASS * c + HALF * u) // 2
-                        nc.tensor.transpose(xt[:, a, u, :], a_words[:, lo : lo + P], ident[:])
-                grouped_a = stage.tile([P, 2 * K_PASS], BF16, name="grouped_a", align_bytes=64)
-                nc.scalar.copy(
-                    out=grouped_a[:].bitcast(F32).rearrange("p (a m u) -> p a m u", a=2, u=2),
-                    in_=xt[:].rearrange("p a u m -> p a m u"),
+            nc.gpsimd.memset(mask_a_f[:], -1.0)
+            for base, fill in ((-1, 65535.0), (0, 0.0)):
+                nc.gpsimd.affine_select(
+                    out=mask_a_f[:], in_=mask_a_f[:], compare_op=ALU.is_ge, fill=fill,
+                    base=base, pattern=[[-2, P // 2]], channel_multiplier=1,
                 )
-                i0 = unit_of[pair[0]]
-                nc.vector.quantize_mx(
-                    out=codes_a[:, i0 : i0 + 2, :].rearrange("p a m -> p (a m)").bitcast(FP8X4),
-                    scales=scales_a[:, i0 : i0 + 2, :].rearrange("p a m -> p (a m)"),
-                    in_=grouped_a[:],
-                )
-            for r in range(BLOCKS_PER_PASS):
-                mi = BLOCKS_PER_PASS * g + r
-                kept = P * (mi + 1)
-                if kept < SIZE:
-                    nc.vector.memset(out_sb[mi][:, kept:], 0.0)
-                for n in range(g + 1):
-                    need = min(K_PASS, kept - K_PASS * n)
-                    wide = need if need in (128, 256, 512) else K_PASS
-                    acc = psum_o.tile([P, K_PASS], F32, name="acc")
-                    for c in range(n, g + 1):
-                        i = unit_of[(mi, c)]
-                        cols = slice(K_PASS * n, K_PASS * n + wide)
-                        nc.tensor.matmul_mx(
-                            out=acc[:, 0:wide],
-                            lhsT=codes_a[:, i, :].bitcast(FP8X4),
-                            lhsT_scale=scales_a[:, i, :],
-                            rhs=codes_b[c][:, cols].bitcast(FP8X4),
-                            rhs_scale=scales_b[c][:, cols],
-                            start=(c == n),
-                            stop=(c == g),
-                        )
-                    nc.scalar.copy(
-                        out=out_sb[mi][:, K_PASS * n : K_PASS * n + need], in_=acc[:, 0:need]
-                    )
-                nc.sync.dma_start(out=out[P * mi : P * (mi + 1), :], in_=out_sb[mi][:])
+            make_identity(nc, ident[:])
+
+        load_b(0)
+        for mi in range(0, 4):
+            load_a(mi)
+        load_b(1)
+        for mi in range(4, 12):
+            load_a(mi)
+        load_b(2)
+
+        nc.vector.memset(zero_src[:], 0.0)
+        build_masks()
+        for mi in range(0, 4):
+            zero_out_scalar(mi)
+        zero_b(0)
+        for mi in range(0, 3):
+            zero_a(mi)
+        nc.vector.tensor_copy(out=mask_b[:], in_=mask_b_f[:])
+        nc.vector.tensor_copy(out=mask_a[:], in_=mask_a_f[:])
+        for mi in range(4, 8):
+            zero_out_vector(mi)
+
+        mask_b_half(0, 0)
+        mask_b_half(0, 1)
+        regroup_b(0, 0)
+        for mi in range(0, 4):
+            mask_a_block(mi)
+        quant_b(0, 0)
+        for pair in (0, 1):
+            transpose_pair(pair)
+            copy_pair(pair)
+        zero_b(1)
+        mask_b_half(1, 0)
+        mask_b_half(1, 1)
+        regroup_b(1, 1, on_scalar=True)
+        quant_pair(0)
+        quant_pair(1)
+        for mi in range(0, 4):
+            products(mi)
+
+        regroup_b(1, 0)
+        for mi in range(4, 7):
+            zero_a(mi)
+        for mi in range(4, 8):
+            mask_a_block(mi)
+        quant_b(1, 0)
+        quant_b(1, 1)
+        for pair in range(2, 6):
+            transpose_pair(pair)
+            copy_pair(pair)
+        for mi in range(8, 11):
+            zero_a(mi)
+        for mi in range(8, 12):
+            mask_a_block(mi)
+        zero_b(2)
+        for pair in range(2, 6):
+            quant_pair(pair)
+        for pair in range(6, 12):
+            transpose_pair(pair)
+            copy_pair(pair)
+        for mi in range(4, 8):
+            products(mi)
+
+        for pair in range(6, 9):
+            quant_pair(pair)
+        mask_b_half(2, 0)
+        mask_b_half(2, 1)
+        regroup_b(2, 0)
+        for pair in range(9, 12):
+            quant_pair(pair)
+        regroup_b(2, 1)
+        quant_b(2, 0)
+        regroup_b(2, 2)
+        quant_b(2, 1)
+        quant_b(2, 2)
+        for mi in range(8, 11):
+            passes(mi, 0, 0, 1)
+            passes(mi, 1, 1, 1)
+        passes(11, 0, 0, 1)
+        for mi in range(8, 12):
+            passes(mi, 0, 2, 2)
+            copy_out(mi, 0)
+            if mi == 11:
+                passes(mi, 1, 1, 1)
+            passes(mi, 1, 2, 2)
+            copy_out(mi, 1, on_vector=True)
+            passes(mi, 2, 2, 2)
+            copy_out(mi, 2, on_vector=(mi < 10))
+            store(mi)

@@ -22,6 +22,9 @@ BLOCKS_PER_PASS = K_PASS // P
 FLOPS = 2 * (SIZE * (SIZE + 1) * (SIZE + 2) // 6)
 BYTES = 2 * (SIZE * (SIZE + 1) // 2) * 2 + SIZE * SIZE * 4
 
+SUPER = 2 * P
+SUPERS = SIZE // SUPER
+
 
 def tile_modelnew_kernel(tc, A, B, out):
     nc = tc.nc
@@ -45,12 +48,12 @@ def tile_modelnew_kernel(tc, A, B, out):
             raw_b.append(keep.tile([P, 4, width], BF16, name="raw_b%d" % c, align_bytes=64))
             codes_b.append(keep.tile([P, width], U32, name="codes_b%d" % c, align_bytes=64))
             scales_b.append(keep.tile([P, width], U8, name="scales_b%d" % c, align_bytes=64))
-        units = [(mi, c) for mi in range(ROW_BLOCKS) for c in range(mi // BLOCKS_PER_PASS + 1)]
-        unit_of = dict((unit, i) for i, unit in enumerate(units))
-        codes_a = keep.tile([P, len(units), P], U32, name="codes_a", align_bytes=64)
-        scales_a = keep.tile([P, len(units), P], U8, name="scales_a", align_bytes=64)
-        out_sb = [keep.tile([P, SIZE], F32, name="out_sb%d" % mi) for mi in range(8)]
-        out_sb.extend(out_sb[0:4])
+        pairs = [(s, c) for s in range(SUPERS) for c in range(s // 2 + 1)]
+        pair_of = dict((pair, i) for i, pair in enumerate(pairs))
+        codes_a = keep.tile([P, len(pairs), 2, P], U32, name="codes_a", align_bytes=64)
+        scales_a = keep.tile([P, len(pairs), 2, P], U8, name="scales_a", align_bytes=64)
+        out_sb = [keep.tile([P, 2, SIZE], F32, name="out_sb%d" % s) for s in range(4)]
+        out_sb.extend(out_sb[0:2])
         ident = const.tile([P, P], F32, name="ident")
         zero_src = const.tile([P, 8], F32, name="zero_src")
         mask_a_f = const.tile([P, P // 2], F32, name="mask_a_f")
@@ -83,14 +86,14 @@ def tile_modelnew_kernel(tc, A, B, out):
         def zero_a(mi):
             nc.vector.memset(raw_a[mi][:].bitcast(I32)[:, P * (mi + 1) // 2 :], 0)
 
-        def zero_out_scalar(mi):
-            kept = P * (mi + 1)
+        def zero_out_scalar(s, j):
+            kept = SUPER * (s + 1)
             nc.scalar.copy(
-                out=out_sb[mi][:, kept:], in_=zero_src[:, 0:1].to_broadcast([P, SIZE - kept])
+                out=out_sb[s][:, j, kept:], in_=zero_src[:, 0:1].to_broadcast([P, SIZE - kept])
             )
 
-        def zero_out_vector(mi):
-            nc.vector.memset(out_sb[mi][:, P * (mi + 1) :], 0.0)
+        def zero_out_vector(s):
+            nc.vector.memset(out_sb[s][:, :, SUPER * (s + 1) :], 0.0)
 
         def mask_b_half(g, u):
             lo = (K_PASS * g + HALF * u) // 2
@@ -120,72 +123,70 @@ def tile_modelnew_kernel(tc, A, B, out):
             diag = raw_a[mi][:].bitcast(I32)[:, P * mi // 2 : P * (mi + 1) // 2]
             nc.vector.tensor_tensor(out=diag, in0=diag, in1=mask_a[:], op=ALU.bitwise_and)
 
-        def transpose_pair(pair):
+        def transpose_a(s, c):
             xt = psum.tile([P, 2, 2, P], F32, name="xt", tag="bank")
-            banks_t[pair] = xt
+            banks_t[(s, c)] = xt
             for a in range(2):
-                mi, c = units[2 * pair + a]
-                a_words = raw_a[mi][:].bitcast(F32)
+                a_words = raw_a[2 * s + a][:].bitcast(F32)
                 for u in range(2):
                     lo = (K_PASS * c + HALF * u) // 2
-                    nc.tensor.transpose(xt[:, a, u, :], a_words[:, lo : lo + P], ident[:])
+                    nc.tensor.transpose(xt[:, u, a, :], a_words[:, lo : lo + P], ident[:])
 
-        def copy_pair(pair, on_vector=False):
+        def copy_a(s, c, on_vector=False):
             grouped = stage_a.tile([P, 2 * K_PASS], BF16, name="grouped_a", align_bytes=64)
-            grouped_a[pair] = grouped
-            dst = grouped[:].bitcast(F32).rearrange("p (a m u) -> p a m u", a=2, u=2)
-            src = banks_t[pair][:].rearrange("p a u m -> p a m u")
+            grouped_a[(s, c)] = grouped
+            dst = grouped[:].bitcast(F32).rearrange("p (j m u) -> p j m u", j=2, u=2)
+            src = banks_t[(s, c)][:].rearrange("p u a (x j) -> p j (a x) u", j=2)
             if on_vector:
                 nc.vector.tensor_copy(out=dst, in_=src)
             else:
                 nc.scalar.copy(out=dst, in_=src)
 
-        def quant_pair(pair):
-            i0 = 2 * pair
+        def quant_a(s, c):
+            i = pair_of[(s, c)]
             nc.vector.quantize_mx(
-                out=codes_a[:, i0 : i0 + 2, :].rearrange("p a m -> p (a m)").bitcast(FP8X4),
-                scales=scales_a[:, i0 : i0 + 2, :].rearrange("p a m -> p (a m)"),
-                in_=grouped_a[pair][:],
+                out=codes_a[:, i, :, :].rearrange("p j m -> p (j m)").bitcast(FP8X4),
+                scales=scales_a[:, i, :, :].rearrange("p j m -> p (j m)"),
+                in_=grouped_a[(s, c)][:],
             )
 
-        def passes(mi, n, first, last):
-            g = mi // BLOCKS_PER_PASS
-            need = min(K_PASS, P * (mi + 1) - K_PASS * n)
-            wide = need if need in (128, 256, 512) else K_PASS
+        def passes(s, j, n, first, last):
+            wide = min(K_PASS, SUPER * (s + 1) - K_PASS * n)
             if first == n:
                 acc = psum.tile([P, K_PASS], F32, name="acc", tag="bank")
-                banks_o[(mi, n)] = acc
-            acc = banks_o[(mi, n)]
+                banks_o[(s, j, n)] = acc
+            acc = banks_o[(s, j, n)]
             cols = slice(K_PASS * n, K_PASS * n + wide)
             for c in range(first, last + 1):
-                i = unit_of[(mi, c)]
+                i = pair_of[(s, c)]
                 nc.tensor.matmul_mx(
                     out=acc[:, 0:wide],
-                    lhsT=codes_a[:, i, :].bitcast(FP8X4),
-                    lhsT_scale=scales_a[:, i, :],
+                    lhsT=codes_a[:, i, j, :].bitcast(FP8X4),
+                    lhsT_scale=scales_a[:, i, j, :],
                     rhs=codes_b[c][:, cols].bitcast(FP8X4),
                     rhs_scale=scales_b[c][:, cols],
                     start=(c == n),
-                    stop=(c == g),
+                    stop=(c == s // 2),
                 )
 
-        def copy_out(mi, n, on_vector=False):
-            need = min(K_PASS, P * (mi + 1) - K_PASS * n)
-            dst = out_sb[mi][:, K_PASS * n : K_PASS * n + need]
+        def copy_out(s, j, n, on_vector=False):
+            wide = min(K_PASS, SUPER * (s + 1) - K_PASS * n)
+            dst = out_sb[s][:, j, K_PASS * n : K_PASS * n + wide]
             if on_vector:
-                nc.vector.tensor_copy(out=dst, in_=banks_o[(mi, n)][:, 0:need])
+                nc.vector.tensor_copy(out=dst, in_=banks_o[(s, j, n)][:, 0:wide])
             else:
-                nc.scalar.copy(out=dst, in_=banks_o[(mi, n)][:, 0:need])
+                nc.scalar.copy(out=dst, in_=banks_o[(s, j, n)][:, 0:wide])
 
-        def store(mi):
-            nc.sync.dma_start(out=out[P * mi : P * (mi + 1), :], in_=out_sb[mi][:])
+        def store(s):
+            rows = out[SUPER * s : SUPER * (s + 1), :].rearrange("(m j) n -> m j n", j=2)
+            nc.sync.dma_start(out=rows, in_=out_sb[s][:])
 
-        def products(mi):
-            g = mi // BLOCKS_PER_PASS
-            for n in range(g + 1):
-                passes(mi, n, n, g)
-                copy_out(mi, n)
-            store(mi)
+        def products(s, vector_tiles=()):
+            for j in range(2):
+                for n in range(s // 2 + 1):
+                    passes(s, j, n, n, s // 2)
+                    copy_out(s, j, n, on_vector=((j, n) in vector_tiles))
+            store(s)
 
         def build_masks():
             nc.gpsimd.memset(mask_b_f[:], -1.0)
@@ -212,33 +213,34 @@ def tile_modelnew_kernel(tc, A, B, out):
 
         nc.vector.memset(zero_src[:], 0.0)
         build_masks()
-        for mi in range(0, 4):
-            zero_out_scalar(mi)
+        for s in range(2):
+            for j in range(2):
+                zero_out_scalar(s, j)
         zero_b(0)
         for mi in range(0, 3):
             zero_a(mi)
         nc.vector.tensor_copy(out=mask_b[:], in_=mask_b_f[:])
-        nc.vector.tensor_copy(out=mask_a[:], in_=mask_a_f[:])
-        for mi in range(4, 8):
-            zero_out_vector(mi)
+        zero_out_vector(2)
+        zero_out_vector(3)
 
         mask_b_half(0, 0)
         mask_b_half(0, 1)
         regroup_b(0, 0)
+        nc.vector.tensor_copy(out=mask_a[:], in_=mask_a_f[:])
         for mi in range(0, 4):
             mask_a_block(mi)
         quant_b(0, 0)
-        for pair in (0, 1):
-            transpose_pair(pair)
-            copy_pair(pair)
+        for s in range(2):
+            transpose_a(s, 0)
+            copy_a(s, 0)
         zero_b(1)
         mask_b_half(1, 0)
         mask_b_half(1, 1)
-        regroup_b(1, 1, on_scalar=True)
-        quant_pair(0)
-        quant_pair(1)
-        for mi in range(0, 4):
-            products(mi)
+        regroup_b(1, 1)
+        quant_a(0, 0)
+        quant_a(1, 0)
+        products(0)
+        products(1)
 
         regroup_b(1, 0)
         for mi in range(4, 7):
@@ -247,45 +249,56 @@ def tile_modelnew_kernel(tc, A, B, out):
             mask_a_block(mi)
         quant_b(1, 0)
         quant_b(1, 1)
-        for pair in range(2, 6):
-            transpose_pair(pair)
-            copy_pair(pair)
+        for s in (2, 3):
+            for c in range(2):
+                transpose_a(s, c)
+                copy_a(s, c)
         for mi in range(8, 11):
             zero_a(mi)
         for mi in range(8, 12):
             mask_a_block(mi)
         zero_b(2)
-        for pair in range(2, 6):
-            quant_pair(pair)
-        for pair in range(6, 12):
-            transpose_pair(pair)
-            copy_pair(pair)
-        for mi in range(4, 8):
-            products(mi)
+        for s in (2, 3):
+            for c in range(2):
+                quant_a(s, c)
+        for c in range(3):
+            transpose_a(4, c)
+            copy_a(4, c)
+        products(2)
+        products(3)
+        for c in range(3):
+            transpose_a(5, c)
+            copy_a(5, c)
 
-        for pair in range(6, 9):
-            quant_pair(pair)
+        quant_a(4, 0)
+        quant_a(4, 1)
         mask_b_half(2, 0)
         mask_b_half(2, 1)
         regroup_b(2, 0)
-        for pair in range(9, 12):
-            quant_pair(pair)
+        quant_a(4, 2)
         regroup_b(2, 1)
         quant_b(2, 0)
         regroup_b(2, 2)
         quant_b(2, 1)
         quant_b(2, 2)
-        for mi in range(8, 11):
-            passes(mi, 0, 0, 1)
-            passes(mi, 1, 1, 1)
-        passes(11, 0, 0, 1)
-        for mi in range(8, 12):
-            passes(mi, 0, 2, 2)
-            copy_out(mi, 0)
-            if mi == 11:
-                passes(mi, 1, 1, 1)
-            passes(mi, 1, 2, 2)
-            copy_out(mi, 1, on_vector=True)
-            passes(mi, 2, 2, 2)
-            copy_out(mi, 2, on_vector=(mi < 10))
-            store(mi)
+        for c in range(3):
+            quant_a(5, c)
+        for j in range(2):
+            passes(4, j, 0, 0, 1)
+        for j in range(2):
+            passes(4, j, 1, 1, 1)
+        for j in range(2):
+            passes(4, j, 0, 2, 2)
+            copy_out(4, j, 0)
+        for j in range(2):
+            passes(4, j, 1, 2, 2)
+            copy_out(4, j, 1)
+        for j in range(2):
+            passes(4, j, 2, 2, 2)
+            copy_out(4, j, 2, on_vector=True)
+        store(4)
+        for j in range(2):
+            for n in range(3):
+                passes(5, j, n, n, 2)
+                copy_out(5, j, n, on_vector=(n == 1))
+        store(5)

@@ -13,17 +13,19 @@ ALU = mybir.AluOpType
 
 SIZE = 1536
 P = 128
-K_PASS = 512
-HALF = 256
-ROW_BLOCKS = SIZE // P
+K_PASS = 4 * P
+HALF = K_PASS // 2
 PASSES = SIZE // K_PASS
-BLOCKS_PER_PASS = K_PASS // P
+STRIPE = 2 * P
+STRIPES = SIZE // STRIPE
+ROW_BLOCKS = SIZE // P
 
 FLOPS = 2 * (SIZE * (SIZE + 1) * (SIZE + 2) // 6)
 BYTES = 2 * (SIZE * (SIZE + 1) // 2) * 2 + SIZE * SIZE * 4
 
-SUPER = 2 * P
-SUPERS = SIZE // SUPER
+
+def last_pass(s):
+    return STRIPE * s // K_PASS
 
 
 def tile_modelnew_kernel(tc, A, B, out):
@@ -37,9 +39,9 @@ def tile_modelnew_kernel(tc, A, B, out):
         ctx.enter_context(tc.manual_schedule())
 
         raw_a = []
-        for mi in range(ROW_BLOCKS):
-            width = K_PASS * (mi // BLOCKS_PER_PASS + 1)
-            raw_a.append(keep.tile([P, width], BF16, name="raw_a%d" % mi, align_bytes=64))
+        for block in range(ROW_BLOCKS):
+            width = K_PASS * (block * P // K_PASS + 1)
+            raw_a.append(keep.tile([P, width], BF16, name="raw_a%d" % block, align_bytes=64))
         raw_b = []
         codes_b = []
         scales_b = []
@@ -48,10 +50,10 @@ def tile_modelnew_kernel(tc, A, B, out):
             raw_b.append(keep.tile([P, 4, width], BF16, name="raw_b%d" % c, align_bytes=64))
             codes_b.append(keep.tile([P, width], U32, name="codes_b%d" % c, align_bytes=64))
             scales_b.append(keep.tile([P, width], U8, name="scales_b%d" % c, align_bytes=64))
-        pairs = [(s, c) for s in range(SUPERS) for c in range(s // 2 + 1)]
-        pair_of = dict((pair, i) for i, pair in enumerate(pairs))
-        codes_a = keep.tile([P, len(pairs), 2, P], U32, name="codes_a", align_bytes=64)
-        scales_a = keep.tile([P, len(pairs), 2, P], U8, name="scales_a", align_bytes=64)
+        pieces = [(s, c) for s in range(STRIPES) for c in range(last_pass(s) + 1)]
+        piece_of = dict((piece, i) for i, piece in enumerate(pieces))
+        codes_a = keep.tile([P, len(pieces), 2, P], U32, name="codes_a", align_bytes=64)
+        scales_a = keep.tile([P, len(pieces), 2, P], U8, name="scales_a", align_bytes=64)
         out_sb = [keep.tile([P, 2, SIZE], F32, name="out_sb%d" % s) for s in range(4)]
         out_sb.extend(out_sb[0:2])
         ident = const.tile([P, P], F32, name="ident")
@@ -65,128 +67,26 @@ def tile_modelnew_kernel(tc, A, B, out):
         banks_t = {}
         banks_o = {}
 
-        def load_b(g):
-            width = K_PASS * (g + 1)
+
+        def load_b(c):
             for u in range(2):
-                cols = width - HALF * (1 - u)
-                rows = B[K_PASS * g + HALF * u : K_PASS * g + HALF * (u + 1), 0:cols]
+                first = K_PASS * c + HALF * u
+                rows = B[first : first + HALF, 0 : first + HALF]
                 nc.sync.dma_start(
-                    out=raw_b[g][:, 2 * u : 2 * u + 2, 0:cols],
-                    in_=rows.rearrange("(q e) w -> q e w", e=2),
+                    out=raw_b[c][:, 2 * u : 2 * u + 2, 0 : first + HALF],
+                    in_=rows.rearrange("(p e) w -> p e w", e=2),
                 )
 
-        def load_a(mi):
-            cols = P * (mi + 1)
-            nc.sync.dma_start(out=raw_a[mi][:, 0:cols], in_=A[P * mi : P * (mi + 1), 0:cols])
-
-        def zero_b(g):
-            width = K_PASS * (g + 1)
-            nc.vector.memset(raw_b[g][:].bitcast(I32)[:, 0:2, (width - HALF) // 2 :], 0)
-
-        def zero_a(mi):
-            nc.vector.memset(raw_a[mi][:].bitcast(I32)[:, P * (mi + 1) // 2 :], 0)
-
-        def zero_out_scalar(s, j):
-            kept = SUPER * (s + 1)
-            nc.scalar.copy(
-                out=out_sb[s][:, j, kept:], in_=zero_src[:, 0:1].to_broadcast([P, SIZE - kept])
+        def load_a(block):
+            cols = P * (block + 1)
+            nc.sync.dma_start(
+                out=raw_a[block][:, 0:cols], in_=A[P * block : P * (block + 1), 0:cols]
             )
-
-        def zero_out_vector(s):
-            nc.vector.memset(out_sb[s][:, :, SUPER * (s + 1) :], 0.0)
-
-        def mask_b_half(g, u):
-            lo = (K_PASS * g + HALF * u) // 2
-            diag = raw_b[g][:].bitcast(I32)[:, 2 * u : 2 * u + 2, lo : lo + P]
-            nc.vector.tensor_tensor(out=diag, in0=diag, in1=mask_b[:], op=ALU.bitwise_and)
-
-        def regroup_b(g, j, on_scalar=False):
-            cols = slice(K_PASS * j, K_PASS * (j + 1))
-            grouped = stage_b.tile([P, 4 * K_PASS], BF16, name="grouped_b", align_bytes=64)
-            grouped_b[(g, j)] = grouped
-            dst = grouped[:].rearrange("p (c i t) -> p c t i", i=4, t=4)
-            src = raw_b[g][:, :, cols].rearrange("p t (c i) -> p c t i", i=4)
-            if on_scalar:
-                nc.scalar.copy(out=dst, in_=src)
-            else:
-                nc.vector.tensor_copy(out=dst, in_=src)
-
-        def quant_b(g, j):
-            cols = slice(K_PASS * j, K_PASS * (j + 1))
-            nc.vector.quantize_mx(
-                out=codes_b[g][:, cols].bitcast(FP8X4),
-                scales=scales_b[g][:, cols],
-                in_=grouped_b[(g, j)][:],
-            )
-
-        def mask_a_block(mi):
-            diag = raw_a[mi][:].bitcast(I32)[:, P * mi // 2 : P * (mi + 1) // 2]
-            nc.vector.tensor_tensor(out=diag, in0=diag, in1=mask_a[:], op=ALU.bitwise_and)
-
-        def transpose_a(s, c):
-            xt = psum.tile([P, 2, 2, P], F32, name="xt", tag="bank")
-            banks_t[(s, c)] = xt
-            for a in range(2):
-                a_words = raw_a[2 * s + a][:].bitcast(F32)
-                for u in range(2):
-                    lo = (K_PASS * c + HALF * u) // 2
-                    nc.tensor.transpose(xt[:, u, a, :], a_words[:, lo : lo + P], ident[:])
-
-        def copy_a(s, c, on_vector=False):
-            grouped = stage_a.tile([P, 2 * K_PASS], BF16, name="grouped_a", align_bytes=64)
-            grouped_a[(s, c)] = grouped
-            dst = grouped[:].bitcast(F32).rearrange("p (j m u) -> p j m u", j=2, u=2)
-            src = banks_t[(s, c)][:].rearrange("p u a (x j) -> p j (a x) u", j=2)
-            if on_vector:
-                nc.vector.tensor_copy(out=dst, in_=src)
-            else:
-                nc.scalar.copy(out=dst, in_=src)
-
-        def quant_a(s, c):
-            i = pair_of[(s, c)]
-            nc.vector.quantize_mx(
-                out=codes_a[:, i, :, :].rearrange("p j m -> p (j m)").bitcast(FP8X4),
-                scales=scales_a[:, i, :, :].rearrange("p j m -> p (j m)"),
-                in_=grouped_a[(s, c)][:],
-            )
-
-        def passes(s, j, n, first, last):
-            wide = min(K_PASS, SUPER * (s + 1) - K_PASS * n)
-            if first == n:
-                acc = psum.tile([P, K_PASS], F32, name="acc", tag="bank")
-                banks_o[(s, j, n)] = acc
-            acc = banks_o[(s, j, n)]
-            cols = slice(K_PASS * n, K_PASS * n + wide)
-            for c in range(first, last + 1):
-                i = pair_of[(s, c)]
-                nc.tensor.matmul_mx(
-                    out=acc[:, 0:wide],
-                    lhsT=codes_a[:, i, j, :].bitcast(FP8X4),
-                    lhsT_scale=scales_a[:, i, j, :],
-                    rhs=codes_b[c][:, cols].bitcast(FP8X4),
-                    rhs_scale=scales_b[c][:, cols],
-                    start=(c == n),
-                    stop=(c == s // 2),
-                )
-
-        def copy_out(s, j, n, on_vector=False):
-            wide = min(K_PASS, SUPER * (s + 1) - K_PASS * n)
-            dst = out_sb[s][:, j, K_PASS * n : K_PASS * n + wide]
-            if on_vector:
-                nc.vector.tensor_copy(out=dst, in_=banks_o[(s, j, n)][:, 0:wide])
-            else:
-                nc.scalar.copy(out=dst, in_=banks_o[(s, j, n)][:, 0:wide])
 
         def store(s):
-            rows = out[SUPER * s : SUPER * (s + 1), :].rearrange("(m j) n -> m j n", j=2)
+            rows = out[STRIPE * s : STRIPE * (s + 1), :].rearrange("(m j) n -> m j n", j=2)
             nc.sync.dma_start(out=rows, in_=out_sb[s][:])
 
-        def products(s, vector_tiles=()):
-            for j in range(2):
-                for n in range(s // 2 + 1):
-                    passes(s, j, n, n, s // 2)
-                    copy_out(s, j, n, on_vector=((j, n) in vector_tiles))
-            store(s)
 
         def build_masks():
             nc.gpsimd.memset(mask_b_f[:], -1.0)
@@ -203,102 +103,187 @@ def tile_modelnew_kernel(tc, A, B, out):
                 )
             make_identity(nc, ident[:])
 
+        def zero_b(c):
+            width = K_PASS * (c + 1)
+            nc.vector.memset(raw_b[c][:].bitcast(I32)[:, 0:2, (width - HALF) // 2 :], 0)
+
+        def zero_a(block):
+            if P * (block + 1) % K_PASS:
+                nc.vector.memset(raw_a[block][:].bitcast(I32)[:, P * (block + 1) // 2 :], 0)
+
+        def zero_out_on_scalar(s):
+            for j in range(2):
+                kept = STRIPE * (s + 1)
+                nc.scalar.copy(
+                    out=out_sb[s][:, j, kept:],
+                    in_=zero_src[:, 0:1].to_broadcast([P, SIZE - kept]),
+                )
+
+        def zero_out_on_vector(s):
+            nc.vector.memset(out_sb[s][:, :, STRIPE * (s + 1) :], 0.0)
+
+        def mask_b_pass(c):
+            for u in range(2):
+                lo = (K_PASS * c + HALF * u) // 2
+                diag = raw_b[c][:].bitcast(I32)[:, 2 * u : 2 * u + 2, lo : lo + P]
+                nc.vector.tensor_tensor(out=diag, in0=diag, in1=mask_b[:], op=ALU.bitwise_and)
+
+        def mask_a_stripe(s):
+            for block in (2 * s, 2 * s + 1):
+                zero_a(block)
+            for block in (2 * s, 2 * s + 1):
+                diag = raw_a[block][:].bitcast(I32)[:, P * block // 2 : P * (block + 1) // 2]
+                nc.vector.tensor_tensor(out=diag, in0=diag, in1=mask_a[:], op=ALU.bitwise_and)
+
+
+        def regroup_b(c, n):
+            cols = slice(K_PASS * n, K_PASS * (n + 1))
+            grouped = stage_b.tile([P, 4 * K_PASS], BF16, name="grouped_b", align_bytes=64)
+            grouped_b[(c, n)] = grouped
+            nc.vector.tensor_copy(
+                out=grouped[:].rearrange("p (w i t) -> p w t i", i=4, t=4),
+                in_=raw_b[c][:, :, cols].rearrange("p t (w i) -> p w t i", i=4),
+            )
+
+        def quantise_b(c, n):
+            cols = slice(K_PASS * n, K_PASS * (n + 1))
+            nc.vector.quantize_mx(
+                out=codes_b[c][:, cols].bitcast(FP8X4),
+                scales=scales_b[c][:, cols],
+                in_=grouped_b[(c, n)][:],
+            )
+
+
+        def transpose_a(s, c):
+            xt = psum.tile([P, 2, 2, P], F32, name="xt", tag="bank")
+            banks_t[(s, c)] = xt
+            for a in range(2):
+                a_words = raw_a[2 * s + a][:].bitcast(F32)
+                for u in range(2):
+                    lo = (K_PASS * c + HALF * u) // 2
+                    nc.tensor.transpose(xt[:, u, a, :], a_words[:, lo : lo + P], ident[:])
+            grouped = stage_a.tile([P, 2 * K_PASS], BF16, name="grouped_a", align_bytes=64)
+            grouped_a[(s, c)] = grouped
+            nc.scalar.copy(
+                out=grouped[:].bitcast(F32).rearrange("p (j m u) -> p j m u", j=2, u=2),
+                in_=xt[:].rearrange("p u a (x j) -> p j (a x) u", j=2),
+            )
+
+        def quantise_a(s, c):
+            i = piece_of[(s, c)]
+            nc.vector.quantize_mx(
+                out=codes_a[:, i, :, :].rearrange("p j m -> p (j m)").bitcast(FP8X4),
+                scales=scales_a[:, i, :, :].rearrange("p j m -> p (j m)"),
+                in_=grouped_a[(s, c)][:],
+            )
+
+
+        def width_of(s, n):
+            return min(K_PASS, STRIPE * (s + 1) - K_PASS * n)
+
+        def multiply(s, j, n, first, last):
+            if first == n:
+                acc = psum.tile([P, K_PASS], F32, name="acc", tag="bank")
+                banks_o[(s, j, n)] = acc
+            cols = slice(K_PASS * n, K_PASS * n + width_of(s, n))
+            for c in range(first, last + 1):
+                i = piece_of[(s, c)]
+                nc.tensor.matmul_mx(
+                    out=banks_o[(s, j, n)][:, 0 : width_of(s, n)],
+                    lhsT=codes_a[:, i, j, :].bitcast(FP8X4),
+                    lhsT_scale=scales_a[:, i, j, :],
+                    rhs=codes_b[c][:, cols].bitcast(FP8X4),
+                    rhs_scale=scales_b[c][:, cols],
+                    start=(c == n),
+                    stop=(c == last_pass(s)),
+                )
+
+        def copy_out(s, j, n, engine):
+            wide = width_of(s, n)
+            dst = out_sb[s][:, j, K_PASS * n : K_PASS * n + wide]
+            if engine == "vector":
+                nc.vector.tensor_copy(out=dst, in_=banks_o[(s, j, n)][:, 0:wide])
+            else:
+                nc.scalar.copy(out=dst, in_=banks_o[(s, j, n)][:, 0:wide])
+
+        def finish(s, first, on_vector=()):
+            for n in range(last_pass(s) + 1):
+                for j in range(2):
+                    multiply(s, j, n, max(first, n), last_pass(s))
+                    copy_out(s, j, n, "vector" if (j, n) in on_vector else "scalar")
+            store(s)
+
+        def start_early(s):
+            for n in range(last_pass(s)):
+                for j in range(2):
+                    multiply(s, j, n, n, last_pass(s) - 1)
+
         load_b(0)
-        for mi in range(0, 4):
-            load_a(mi)
+        for block in range(0, 4):
+            load_a(block)
         load_b(1)
-        for mi in range(4, 12):
-            load_a(mi)
+        for block in range(4, ROW_BLOCKS):
+            load_a(block)
         load_b(2)
 
         nc.vector.memset(zero_src[:], 0.0)
         build_masks()
-        for s in range(2):
-            for j in range(2):
-                zero_out_scalar(s, j)
+        zero_out_on_scalar(0)
+        zero_out_on_scalar(1)
         zero_b(0)
-        for mi in range(0, 3):
-            zero_a(mi)
         nc.vector.tensor_copy(out=mask_b[:], in_=mask_b_f[:])
-        zero_out_vector(2)
-        zero_out_vector(3)
+        zero_out_on_vector(2)
+        zero_out_on_vector(3)
 
-        mask_b_half(0, 0)
-        mask_b_half(0, 1)
+        mask_b_pass(0)
         regroup_b(0, 0)
         nc.vector.tensor_copy(out=mask_a[:], in_=mask_a_f[:])
-        for mi in range(0, 4):
-            mask_a_block(mi)
-        quant_b(0, 0)
-        for s in range(2):
-            transpose_a(s, 0)
-            copy_a(s, 0)
+        mask_a_stripe(0)
+        mask_a_stripe(1)
+        quantise_b(0, 0)
+        transpose_a(0, 0)
+        transpose_a(1, 0)
         zero_b(1)
-        mask_b_half(1, 0)
-        mask_b_half(1, 1)
-        regroup_b(1, 1)
-        quant_a(0, 0)
-        quant_a(1, 0)
-        products(0)
-        products(1)
-
+        mask_b_pass(1)
         regroup_b(1, 0)
-        for mi in range(4, 7):
-            zero_a(mi)
-        for mi in range(4, 8):
-            mask_a_block(mi)
-        quant_b(1, 0)
-        quant_b(1, 1)
+        quantise_a(0, 0)
+        quantise_a(1, 0)
+        finish(0, 0)
+        finish(1, 0)
+
+        regroup_b(1, 1)
+        mask_a_stripe(2)
+        mask_a_stripe(3)
+        quantise_b(1, 0)
+        quantise_b(1, 1)
         for s in (2, 3):
             for c in range(2):
                 transpose_a(s, c)
-                copy_a(s, c)
-        for mi in range(8, 11):
-            zero_a(mi)
-        for mi in range(8, 12):
-            mask_a_block(mi)
+        mask_a_stripe(4)
+        mask_a_stripe(5)
         zero_b(2)
         for s in (2, 3):
             for c in range(2):
-                quant_a(s, c)
-        for c in range(3):
+                quantise_a(s, c)
+        for c in range(PASSES):
             transpose_a(4, c)
-            copy_a(4, c)
-        products(2)
-        products(3)
-        for c in range(3):
+        finish(2, 0)
+        finish(3, 0)
+        for c in range(PASSES):
             transpose_a(5, c)
-            copy_a(5, c)
 
-        quant_a(4, 0)
-        quant_a(4, 1)
-        mask_b_half(2, 0)
-        mask_b_half(2, 1)
+        quantise_a(4, 0)
+        quantise_a(4, 1)
+        mask_b_pass(2)
         regroup_b(2, 0)
-        quant_a(4, 2)
+        quantise_a(4, 2)
         regroup_b(2, 1)
-        quant_b(2, 0)
+        quantise_b(2, 0)
         regroup_b(2, 2)
-        quant_b(2, 1)
-        quant_b(2, 2)
-        for c in range(3):
-            quant_a(5, c)
-        for j in range(2):
-            passes(4, j, 0, 0, 1)
-        for j in range(2):
-            passes(4, j, 1, 1, 1)
-        for j in range(2):
-            passes(4, j, 0, 2, 2)
-            copy_out(4, j, 0)
-        for j in range(2):
-            passes(4, j, 1, 2, 2)
-            copy_out(4, j, 1)
-        for j in range(2):
-            passes(4, j, 2, 2, 2)
-            copy_out(4, j, 2, on_vector=True)
-        store(4)
-        for j in range(2):
-            for n in range(3):
-                passes(5, j, n, n, 2)
-                copy_out(5, j, n, on_vector=(n == 1))
-        store(5)
+        quantise_b(2, 1)
+        quantise_b(2, 2)
+        for c in range(PASSES):
+            quantise_a(5, c)
+        start_early(4)
+        finish(4, 2, on_vector=((0, 2), (1, 2)))
+        finish(5, 0, on_vector=((1, 0), (1, 1), (1, 2)))

from contextlib import ExitStack

import concourse.mybir as mybir
from concourse.masks import make_identity

BF16 = mybir.dt.bfloat16
F32 = mybir.dt.float32
I32 = mybir.dt.int32
U32 = mybir.dt.uint32
U8 = mybir.dt.uint8
FP8X4 = mybir.dt.float8_e4m3fn_x4
ALU = mybir.AluOpType

SIZE = 1536
P = 128
K_PASS = 4 * P
HALF = K_PASS // 2
PASSES = SIZE // K_PASS
STRIPE = 2 * P
STRIPES = SIZE // STRIPE
ROW_BLOCKS = SIZE // P

FLOPS = 2 * (SIZE * (SIZE + 1) * (SIZE + 2) // 6)
BYTES = 2 * (SIZE * (SIZE + 1) // 2) * 2 + SIZE * SIZE * 4


def last_pass(s):
    return STRIPE * s // K_PASS


def tile_modelnew_kernel(tc, A, B, out):
    nc = tc.nc
    with ExitStack() as ctx:
        const = ctx.enter_context(tc.tile_pool(name="const", bufs=1))
        keep = ctx.enter_context(tc.tile_pool(name="keep", bufs=1))
        stage_b = ctx.enter_context(tc.tile_pool(name="stage_b", bufs=3))
        stage_a = ctx.enter_context(tc.tile_pool(name="stage_a", bufs=6))
        psum = ctx.enter_context(tc.psum_pool(name="psum", bufs=8))
        ctx.enter_context(tc.manual_schedule())

        raw_a = []
        for block in range(ROW_BLOCKS):
            width = K_PASS * (block * P // K_PASS + 1)
            raw_a.append(keep.tile([P, width], BF16, name="raw_a%d" % block, align_bytes=64))
        raw_b = []
        codes_b = []
        scales_b = []
        for c in range(PASSES):
            width = K_PASS * (c + 1)
            raw_b.append(keep.tile([P, 4, width], BF16, name="raw_b%d" % c, align_bytes=64))
            codes_b.append(keep.tile([P, width], U32, name="codes_b%d" % c, align_bytes=64))
            scales_b.append(keep.tile([P, width], U8, name="scales_b%d" % c, align_bytes=64))
        pieces = [(s, c) for s in range(STRIPES) for c in range(last_pass(s) + 1)]
        piece_of = dict((piece, i) for i, piece in enumerate(pieces))
        codes_a = keep.tile([P, len(pieces), 2, P], U32, name="codes_a", align_bytes=64)
        scales_a = keep.tile([P, len(pieces), 2, P], U8, name="scales_a", align_bytes=64)
        out_sb = [keep.tile([P, 2, SIZE], F32, name="out_sb%d" % s) for s in range(4)]
        out_sb.extend(out_sb[0:2])
        ident = const.tile([P, P], F32, name="ident")
        zero_src = const.tile([P, 8], F32, name="zero_src")
        mask_a_f = const.tile([P, P // 2], F32, name="mask_a_f")
        mask_b_f = const.tile([P, 2, P], F32, name="mask_b_f")
        mask_a = const.tile([P, P // 2], I32, name="mask_a")
        mask_b = const.tile([P, 2, P], I32, name="mask_b")
        grouped_b = {}
        grouped_a = {}
        banks_t = {}
        banks_o = {}


        def load_b(c):
            for u in range(2):
                first = K_PASS * c + HALF * u
                rows = B[first : first + HALF, 0 : first + HALF]
                nc.sync.dma_start(
                    out=raw_b[c][:, 2 * u : 2 * u + 2, 0 : first + HALF],
                    in_=rows.rearrange("(p e) w -> p e w", e=2),
                )

        def load_a(block):
            cols = P * (block + 1)
            nc.sync.dma_start(
                out=raw_a[block][:, 0:cols], in_=A[P * block : P * (block + 1), 0:cols]
            )

        def store(s):
            rows = out[STRIPE * s : STRIPE * (s + 1), :].rearrange("(m j) n -> m j n", j=2)
            nc.sync.dma_start(out=rows, in_=out_sb[s][:])


        def build_masks():
            nc.gpsimd.memset(mask_b_f[:], -1.0)
            for base, fill in ((-1, 65535.0), (0, 0.0)):
                nc.gpsimd.affine_select(
                    out=mask_b_f[:], in_=mask_b_f[:], compare_op=ALU.is_ge, fill=fill,
                    base=base, pattern=[[1, 2], [-2, P]], channel_multiplier=2,
                )
            nc.gpsimd.memset(mask_a_f[:], -1.0)
            for base, fill in ((-1, 65535.0), (0, 0.0)):
                nc.gpsimd.affine_select(
                    out=mask_a_f[:], in_=mask_a_f[:], compare_op=ALU.is_ge, fill=fill,
                    base=base, pattern=[[-2, P // 2]], channel_multiplier=1,
                )
            make_identity(nc, ident[:])

        def zero_b(c):
            width = K_PASS * (c + 1)
            nc.vector.memset(raw_b[c][:].bitcast(I32)[:, 0:2, (width - HALF) // 2 :], 0)

        def zero_a(block):
            if P * (block + 1) % K_PASS:
                nc.vector.memset(raw_a[block][:].bitcast(I32)[:, P * (block + 1) // 2 :], 0)

        def zero_out_on_scalar(s):
            for j in range(2):
                kept = STRIPE * (s + 1)
                nc.scalar.copy(
                    out=out_sb[s][:, j, kept:],
                    in_=zero_src[:, 0:1].to_broadcast([P, SIZE - kept]),
                )

        def zero_out_on_vector(s):
            nc.vector.memset(out_sb[s][:, :, STRIPE * (s + 1) :], 0.0)

        def mask_b_pass(c):
            for u in range(2):
                lo = (K_PASS * c + HALF * u) // 2
                diag = raw_b[c][:].bitcast(I32)[:, 2 * u : 2 * u + 2, lo : lo + P]
                nc.vector.tensor_tensor(out=diag, in0=diag, in1=mask_b[:], op=ALU.bitwise_and)

        def mask_a_stripe(s):
            for block in (2 * s, 2 * s + 1):
                zero_a(block)
            for block in (2 * s, 2 * s + 1):
                diag = raw_a[block][:].bitcast(I32)[:, P * block // 2 : P * (block + 1) // 2]
                nc.vector.tensor_tensor(out=diag, in0=diag, in1=mask_a[:], op=ALU.bitwise_and)


        def regroup_b(c, n):
            cols = slice(K_PASS * n, K_PASS * (n + 1))
            grouped = stage_b.tile([P, 4 * K_PASS], BF16, name="grouped_b", align_bytes=64)
            grouped_b[(c, n)] = grouped
            nc.vector.tensor_copy(
                out=grouped[:].rearrange("p (w i t) -> p w t i", i=4, t=4),
                in_=raw_b[c][:, :, cols].rearrange("p t (w i) -> p w t i", i=4),
            )

        def quantise_b(c, n):
            cols = slice(K_PASS * n, K_PASS * (n + 1))
            nc.vector.quantize_mx(
                out=codes_b[c][:, cols].bitcast(FP8X4),
                scales=scales_b[c][:, cols],
                in_=grouped_b[(c, n)][:],
            )


        def transpose_a(s, c):
            xt = psum.tile([P, 2, 2, P], F32, name="xt", tag="bank")
            banks_t[(s, c)] = xt
            for a in range(2):
                a_words = raw_a[2 * s + a][:].bitcast(F32)
                for u in range(2):
                    lo = (K_PASS * c + HALF * u) // 2
                    nc.tensor.transpose(xt[:, u, a, :], a_words[:, lo : lo + P], ident[:])
            grouped = stage_a.tile([P, 2 * K_PASS], BF16, name="grouped_a", align_bytes=64)
            grouped_a[(s, c)] = grouped
            nc.scalar.copy(
                out=grouped[:].bitcast(F32).rearrange("p (j m u) -> p j m u", j=2, u=2),
                in_=xt[:].rearrange("p u a (x j) -> p j (a x) u", j=2),
            )

        def quantise_a(s, c):
            i = piece_of[(s, c)]
            nc.vector.quantize_mx(
                out=codes_a[:, i, :, :].rearrange("p j m -> p (j m)").bitcast(FP8X4),
                scales=scales_a[:, i, :, :].rearrange("p j m -> p (j m)"),
                in_=grouped_a[(s, c)][:],
            )


        def width_of(s, n):
            return min(K_PASS, STRIPE * (s + 1) - K_PASS * n)

        def multiply(s, j, n, first, last):
            if first == n:
                acc = psum.tile([P, K_PASS], F32, name="acc", tag="bank")
                banks_o[(s, j, n)] = acc
            cols = slice(K_PASS * n, K_PASS * n + width_of(s, n))
            for c in range(first, last + 1):
                i = piece_of[(s, c)]
                nc.tensor.matmul_mx(
                    out=banks_o[(s, j, n)][:, 0 : width_of(s, n)],
                    lhsT=codes_a[:, i, j, :].bitcast(FP8X4),
                    lhsT_scale=scales_a[:, i, j, :],
                    rhs=codes_b[c][:, cols].bitcast(FP8X4),
                    rhs_scale=scales_b[c][:, cols],
                    start=(c == n),
                    stop=(c == last_pass(s)),
                )

        def copy_out(s, j, n, engine):
            wide = width_of(s, n)
            dst = out_sb[s][:, j, K_PASS * n : K_PASS * n + wide]
            if engine == "vector":
                nc.vector.tensor_copy(out=dst, in_=banks_o[(s, j, n)][:, 0:wide])
            else:
                nc.scalar.copy(out=dst, in_=banks_o[(s, j, n)][:, 0:wide])

        def finish(s, first, on_vector=()):
            for n in range(last_pass(s) + 1):
                for j in range(2):
                    multiply(s, j, n, max(first, n), last_pass(s))
                    copy_out(s, j, n, "vector" if (j, n) in on_vector else "scalar")
            store(s)

        def start_early(s):
            for n in range(last_pass(s)):
                for j in range(2):
                    multiply(s, j, n, n, last_pass(s) - 1)

        load_b(0)
        for block in range(0, 4):
            load_a(block)
        load_b(1)
        for block in range(4, ROW_BLOCKS):
            load_a(block)
        load_b(2)

        nc.vector.memset(zero_src[:], 0.0)
        build_masks()
        zero_out_on_scalar(0)
        zero_out_on_scalar(1)
        zero_b(0)
        nc.vector.tensor_copy(out=mask_b[:], in_=mask_b_f[:])
        zero_out_on_vector(2)
        zero_out_on_vector(3)

        mask_b_pass(0)
        regroup_b(0, 0)
        nc.vector.tensor_copy(out=mask_a[:], in_=mask_a_f[:])
        mask_a_stripe(0)
        mask_a_stripe(1)
        quantise_b(0, 0)
        transpose_a(0, 0)
        transpose_a(1, 0)
        zero_b(1)
        mask_b_pass(1)
        regroup_b(1, 0)
        quantise_a(0, 0)
        quantise_a(1, 0)
        finish(0, 0)
        finish(1, 0)

        regroup_b(1, 1)
        mask_a_stripe(2)
        mask_a_stripe(3)
        quantise_b(1, 0)
        quantise_b(1, 1)
        for s in (2, 3):
            for c in range(2):
                transpose_a(s, c)
        mask_a_stripe(4)
        mask_a_stripe(5)
        zero_b(2)
        for s in (2, 3):
            for c in range(2):
                quantise_a(s, c)
        for c in range(PASSES):
            transpose_a(4, c)
        finish(2, 0)
        finish(3, 0)
        for c in range(PASSES):
            transpose_a(5, c)

        quantise_a(4, 0)
        quantise_a(4, 1)
        mask_b_pass(2)
        regroup_b(2, 0)
        quantise_a(4, 2)
        regroup_b(2, 1)
        quantise_b(2, 0)
        regroup_b(2, 2)
        quantise_b(2, 1)
        quantise_b(2, 2)
        for c in range(PASSES):
            quantise_a(5, c)
        start_early(4)
        finish(4, 2, on_vector=((0, 2), (1, 2)))
        finish(5, 0, on_vector=((1, 0), (1, 1), (1, 2)))
